import numpy as np
import ml_dtypes


def mxq(x, axis, fmt="e4m3"):
    dtype, down = {"e4m3": (ml_dtypes.float8_e4m3fn, 7), "e5m2": (ml_dtypes.float8_e5m2, 14)}[fmt]
    v = np.moveaxis(np.asarray(x, np.float32).astype(ml_dtypes.bfloat16).astype(np.float64), axis, -1)
    blocks = v.reshape(v.shape[:-1] + (-1, 32))
    amax = np.abs(blocks).max(-1, keepdims=True)
    byte = np.maximum(np.where(amax > 0, np.frexp(amax)[1] - 1 + 127, 0) - down, 1)
    scale = np.exp2(byte - 127.0)
    codes = (blocks / scale).astype(np.float32).astype(dtype).astype(np.float64)
    return np.moveaxis((codes * scale).reshape(v.shape), -1, axis)


WIDE = False


def mx_kscale(k):
    if not WIDE:
        return np.ones(k)
    levels = np.array([10, -10, 5, -5, 0])
    if k % 512:
        return np.exp2(np.random.permutation(np.resize(levels, k // 32))).repeat(32)
    a = np.empty((k // 512, 16))
    for p in range(k // 512):
        a[p, :8] = np.random.permutation(np.resize(levels, 8))
        for g in range(8):
            far = levels[np.abs(levels - a[p, g]) >= 10]
            a[p, g + 8] = far[np.random.randint(len(far))]
    return np.exp2(a.ravel()).repeat(32)


BF16 = ml_dtypes.bfloat16


def bf(x):
    return np.asarray(x, np.float32).astype(BF16)


def f64(x):
    return np.asarray(x).astype(np.float64)


S, HID, NH, Q_LORA, KV_LORA, NOPE, ROPE, VDIM, BLK = 8192, 512, 4, 1536, 512, 64, 64, 64, 128
EPS = 1e-6


def blockscale(rows, cols, k, g):
    return bf((np.random.random((rows, cols)) * 0.8 + 0.2) * g / np.sqrt(k))


def dequant(w, s):
    so = np.repeat(s, BLK, axis=0)[: w.shape[0]]
    se = np.repeat(so, BLK, axis=1)[:, : w.shape[1]]
    return w * se


def rmsnorm(x, w):
    var = np.mean(x * x, axis=-1, keepdims=True)
    return x * (1.0 / np.sqrt(var + EPS)) * w


def draw0():
    s, t = mx_kscale(HID), mx_kscale(KV_LORA)
    return {"hidden_states": bf(np.random.standard_normal((S, HID)) * s),
            "wkv_a_lat": bf(np.random.standard_normal((KV_LORA, HID)) / s[None, :]),
            "skv_a_lat": blockscale(KV_LORA // BLK, HID // BLK, HID, 1.0),
            "wkv_b": bf(np.random.standard_normal((NH * (NOPE + VDIM), KV_LORA)) / t[None, :]),
            "skv_b": blockscale(NH * (NOPE + VDIM) // BLK, KV_LORA // BLK, KV_LORA, 2.0),
            "kv_ln_w": bf((1.0 + 0.1 * np.random.standard_normal(KV_LORA)) * t)}


def core(hidden_states, wkv_a_lat, skv_a_lat, wkv_b, skv_b, kv_ln_w):
    wa = dequant(f64(wkv_a_lat), f64(skv_a_lat))
    lkv = mxq(f64(hidden_states), 1, "e4m3") @ mxq(wa, 1, "e4m3").T
    kv_nope = rmsnorm(lkv, f64(kv_ln_w))
    wb = dequant(f64(wkv_b), f64(skv_b))
    kvb = (mxq(kv_nope, 1, "e4m3") @ mxq(wb, 1, "e4m3").T).reshape(S, NH, NOPE + VDIM)
    return kvb[..., :NOPE], kvb[..., NOPE:]


def e4m3fn_bytes(y):
    return np.clip(np.asarray(y, np.float64), -448.0, 448.0).astype(np.float32).astype(ml_dtypes.float8_e4m3fn).view(np.uint8)


def e4m3fn_values(b):
    return np.asarray(b, np.uint8).view(ml_dtypes.float8_e4m3fn).astype(np.float64)


def setup_inputs():
    d = draw0()
    x0 = np.asarray(d['hidden_states']).astype(np.float64)
    s = (np.max(np.abs(x0), axis=(0,), keepdims=True) / 448.0).astype(np.float32)
    out = {}
    for k, v in d.items():
        if k == 'hidden_states':
            out['hidden_states_bytes'] = e4m3fn_bytes(x0 / s.astype(np.float64))
            out['hidden_states_scale'] = s
        else:
            out[k] = v
    return out


def reference(hidden_states_bytes, hidden_states_scale, wkv_a_lat, skv_a_lat, wkv_b, skv_b, kv_ln_w):
    return core(e4m3fn_values(hidden_states_bytes) * hidden_states_scale.astype(np.float64), wkv_a_lat, skv_a_lat, wkv_b, skv_b, kv_ln_w)

@@ -1,0 +1,245 @@
+from contextlib import ExitStack
+
+import concourse.mybir as mybir
+from concourse.masks import make_identity
+
+S, HID, LAT, OUT = 8192, 512, 512, 512
+EPS = 1e-6
+FLOPS = 2 * S * HID * LAT + 2 * S * LAT * OUT
+
+F32 = mybir.dt.float32
+BF16 = mybir.dt.bfloat16
+U32 = mybir.dt.uint32
+U8 = mybir.dt.uint8
+E4M3 = mybir.dt.float8_e4m3fn
+FP8X4 = mybir.dt.float8_e4m3fn_x4
+ACT = mybir.ActivationFunctionType
+MULT = mybir.AluOpType.mult
+
+P = 128
+PER = 8
+GROUPS = S // (P * PER)
+PAIRS = S // (2 * P)
+PAIRS_G = PER // 2
+
+
+def tile_deepseekv3attention_pb_t_kernel(
+    tc, hidden_states_bytes, hidden_states_scale, wkv_a_lat, skv_a_lat, wkv_b, skv_b, kv_ln_w, out_0, out_1
+):
+    nc = tc.nc
+    x_hbm = hidden_states_bytes.rearrange("(g p j) k -> g p j k", p=P, j=PER)
+    o_hbm = [
+        o.rearrange("(g p j) h d -> g p j (h d)", p=P, j=PER) for o in (out_0, out_1)
+    ]
+
+    with ExitStack() as ctx:
+        keep = ctx.enter_context(tc.tile_pool(name="keep", bufs=1))
+        ring = ctx.enter_context(tc.tile_pool(name="ring", bufs=3))
+        psum = ctx.enter_context(tc.psum_pool(name="psum", bufs=1))
+        ctx.enter_context(tc.manual_schedule())
+
+        x_bytes = keep.tile([P, GROUPS, PER, HID], U8, align_bytes=64)
+        nc.sync.dma_start(out=x_bytes[:, 0, 0:2, :], in_=x_hbm[0][:, 0:2, :])
+        wa_raw = keep.tile([P, 4, HID], BF16, align_bytes=64)
+        nc.sync.dma_start(out=wa_raw[:], in_=wkv_a_lat.rearrange("(b q) k -> q b k", q=P))
+        k_scale = keep.tile([P, 4], F32)
+        nc.scalar.dma_start(out=k_scale[:], in_=hidden_states_scale.rearrange("o (p t) -> p (o t)", t=4))
+        skv_a_row = keep.tile([P, 16], BF16)
+        nc.scalar.dma_start(out=skv_a_row[:], in_=skv_a_lat.rearrange("b g -> (b g)").partition_broadcast(P))
+        nc.sync.dma_start(out=x_bytes[:, 0, 2:PER, :], in_=x_hbm[0][:, 2:PER, :])
+        wb_raw = keep.tile([P, 4, LAT], BF16, align_bytes=64)
+        nc.sync.dma_start(out=wb_raw[:], in_=wkv_b.rearrange("(b q) k -> q b k", q=P))
+        skv_b_row = keep.tile([P, 16], BF16)
+        nc.scalar.dma_start(out=skv_b_row[:], in_=skv_b.rearrange("b g -> (b g)").partition_broadcast(P))
+        gain_row = keep.tile([P, LAT], BF16)
+        nc.scalar.dma_start(out=gain_row[:], in_=kv_ln_w.partition_broadcast(P))
+        for g in range(1, GROUPS):
+            nc.sync.dma_start(out=x_bytes[:, g, :, :], in_=x_hbm[g])
+
+        ident = keep.tile([P, P], F32)
+        make_identity(nc, ident[:])
+        eps = keep.tile([P, 1], F32)
+        nc.vector.memset(eps[:], EPS)
+        warm = keep.tile([P, 1], F32)
+        nc.scalar.activation(out=warm[:], in_=eps[:], func=ACT.Abs_reciprocal_sqrt, bias=eps[:, 0:1])
+        ident_a = keep.tile([P, P], F32)
+        nc.gpsimd.tensor_copy(
+            out=ident_a[:].rearrange("p (al m ep) -> p al m ep", al=2, ep=2),
+            in_=ident[:].rearrange("p (m al ep) -> p al m ep", al=2, ep=2),
+        )
+        s_a = keep.tile([P, 4], F32)
+        s_b = keep.tile([P, 4], F32)
+        for s_col, row in ((s_a, skv_a_row), (s_b, skv_b_row)):
+            for q in range(4):
+                rows = slice(32 * q, 32 * q + 32)
+                nc.gpsimd.tensor_copy(out=s_col[rows, :], in_=row[rows, q::4])
+        gain = keep.tile([P, LAT], F32)
+        nc.gpsimd.tensor_copy(
+            out=gain[:].rearrange("p (al m ep) -> p al m ep", al=2, ep=2),
+            in_=gain_row[:].rearrange("p (m al ep) -> p al m ep", al=2, ep=2),
+        )
+
+        def weight_transposes(raw, tag, identity):
+            words = raw[:].bitcast(F32)
+            banks = []
+            for half in range(2):
+                bank = psum.tile([P, 2, 2, P], F32, name=tag, tag=tag, bufs=4 if tag == "c" else 2)
+                for h in range(2):
+                    for u in range(2):
+                        nc.tensor.transpose(bank[:, h, u, :], words[:, 2 * half + h, u::2], identity[:])
+                banks.append(bank)
+            return banks
+
+        def weight_scale(banks, s_col, grouped):
+            for b in range(4):
+                src = banks[b // 2][:, b % 2, :, :].bitcast(BF16)
+                for a in range(2):
+                    n0 = 256 * a + 64 * b
+                    part = src[:, :, 128 * a : 128 * a + 128].rearrange("p u (n e) -> p n u e", e=2)
+                    dst = grouped[:, n0 : n0 + 64, :].rearrange("p n (u e) -> p n u e", e=2)
+                    if a == 0:
+                        nc.scalar.activation(out=dst, in_=part, func=ACT.Copy, scale=s_col[:, b : b + 1])
+                    else:
+                        nc.vector.tensor_scalar(out=dst, in0=part, scalar1=s_col[:, b : b + 1], scalar2=None, op0=MULT)
+
+        def weight_quantize(grouped, codes, scales):
+            nc.vector.quantize_mx(
+                out=codes[:].bitcast(FP8X4), scales=scales[:], in_=grouped[:].rearrange("p n t -> p (n t)")
+            )
+
+        wa_grouped = keep.tile([P, LAT, 4], BF16, align_bytes=64)
+        wa_codes = keep.tile([P, LAT], U32, align_bytes=64)
+        wa_scales = keep.tile([P, LAT], U8, align_bytes=64)
+        wb_grouped = keep.tile([P, OUT, 4], BF16, align_bytes=64)
+        wb_codes = keep.tile([P, OUT], U32, align_bytes=64)
+        wb_scales = keep.tile([P, OUT], U8, align_bytes=64)
+
+        st = {}
+
+        def widen(k):
+            g, j = divmod(k, PAIRS_G)
+            xb = ring.tile([P, 2 * HID], BF16, name="xb", bufs=3, align_bytes=64)
+            src = x_bytes[:, g, 2 * j : 2 * j + 2, :].rearrange("p j k -> p (j k)").bitcast(E4M3)
+            if k == 0:
+                nc.vector.tensor_copy(out=xb[:], in_=src)
+            else:
+                nc.gpsimd.tensor_copy(out=xb[:], in_=src)
+            st["xb", k] = xb
+
+        def x_transposes(k):
+            words = st.pop(("xb", k))[:].bitcast(F32).rearrange("p (j w) -> p j w", j=2)
+            xt = psum.tile([P, 2, 2 * P], F32, name="xt", bufs=1)
+            for j in range(2):
+                for u in range(2):
+                    nc.tensor.transpose(xt[:, u, P * j : P * j + P], words[:, j, u::2], ident[:])
+            st["xt", k] = xt
+
+        def x_scale(k):
+            xt = st.pop(("xt", k))
+            xg = ring.tile([P, 2 * P, 4], BF16, name="xg", bufs=2, align_bytes=64)
+            nc.vector.tensor_tensor(
+                out=xg[:].rearrange("p r (u e) -> p r u e", e=2),
+                in0=xt[:].bitcast(BF16).rearrange("p u (r e) -> p r u e", e=2),
+                in1=k_scale[:].rearrange("p (u e) -> p u e", e=2).unsqueeze(1).to_broadcast([P, 2 * P, 2, 2]),
+                op=MULT,
+            )
+            st["xg", k] = xg
+
+        def quantize(k, src, dst):
+            grouped = st.pop((src, k))
+            codes = ring.tile([P, 2 * P], U32, name=dst + "c", bufs=2, align_bytes=64)
+            scales = ring.tile([P, 2 * P], U8, name=dst + "s", bufs=2, align_bytes=64)
+            nc.vector.quantize_mx(
+                out=codes[:].bitcast(FP8X4), scales=scales[:], in_=grouped[:].rearrange("p r t -> p (r t)")
+            )
+            st[dst, k] = (codes, scales)
+
+        def multiply(k, src, w_codes, w_scales, dst, bufs):
+            codes, scales = st.pop((src, k))
+            res = []
+            for j in range(2):
+                cols = slice(P * j, P * j + P)
+                acc = psum.tile([P, 512], F32, name=dst, bufs=bufs)
+                nc.tensor.matmul_mx(
+                    out=acc[:],
+                    lhsT=codes[:, cols].bitcast(FP8X4),
+                    lhsT_scale=scales[:, cols],
+                    rhs=w_codes[:].bitcast(FP8X4),
+                    rhs_scale=w_scales[:],
+                    start=True,
+                    stop=True,
+                )
+                res.append(acc)
+            st[dst, k] = res
+
+        def square_sums(k):
+            junk = ring.tile([P, LAT], BF16, name="junk", bufs=2)
+            ssq = ring.tile([P, 2], F32, name="ssq", bufs=3)
+            rstd = ring.tile([P, 2], F32, name="rstd", bufs=3)
+            for j in range(2):
+                nc.scalar.activation(
+                    out=junk[:], in_=st["c", k][j][:], func=ACT.Square, accum_out=ssq[:, j : j + 1]
+                )
+            nc.scalar.activation(
+                out=rstd[:], in_=ssq[:], func=ACT.Abs_reciprocal_sqrt, scale=1.0 / LAT, bias=eps[:, 0:1]
+            )
+            st["rstd", k] = rstd
+
+        def norm(k):
+            rstd = st.pop(("rstd", k))
+            h = ring.tile([P, 2, LAT], BF16, name="h", bufs=2, align_bytes=64)
+            for j, acc in enumerate(st.pop(("c", k))):
+                nc.vector.scalar_tensor_tensor(
+                    out=h[:, j, :], in0=acc[:], scalar=rstd[:, j : j + 1], in1=gain[:], op0=MULT, op1=MULT
+                )
+            st["h", k] = h
+
+        def h_transposes(k):
+            words = st.pop(("h", k))[:].bitcast(F32)
+            ht = psum.tile([P, 2, 2 * P], F32, name="ht", bufs=1)
+            for j in range(2):
+                for u in range(2):
+                    nc.tensor.transpose(ht[:, u, P * j : P * j + P], words[:, j, P * u : P * u + P], ident[:])
+            st["ht", k] = ht
+
+        def h_group(k):
+            ht = st.pop(("ht", k))
+            hg = ring.tile([P, 2 * P, 4], BF16, name="hg", bufs=2, align_bytes=64)
+            nc.scalar.copy(out=hg[:].bitcast(F32), in_=ht[:].rearrange("p u r -> p r u"))
+            st["hg", k] = hg
+
+        def finish(k):
+            g, i = divmod(k, PAIRS_G)
+            res = ring.tile([P, 2, 2, 256], F32, name="res", bufs=3)
+            for j, acc in enumerate(st.pop(("o", k))):
+                nc.scalar.copy(out=res[:, :, j, :], in_=acc[:].rearrange("p (h n) -> p h n", h=2))
+            for half in range(2):
+                nc.sync.dma_start(out=o_hbm[half][g][:, 2 * i : 2 * i + 2, :], in_=res[:, half, :, :])
+
+        def stage(fn, k, *args):
+            if 0 <= k < PAIRS:
+                fn(k, *args)
+
+        for k in range(-3, PAIRS + 3):
+            stage(widen, k + 3)
+            if k == -1:
+                wa_banks = weight_transposes(wa_raw, "c", ident_a)
+            stage(quantize, k, "xg", "xq")
+            stage(quantize, k - 3, "hg", "hq")
+            stage(multiply, k, "xq", wa_codes, wa_scales, "c", 4)
+            stage(multiply, k - 3, "hq", wb_codes, wb_scales, "o", 2)
+            stage(x_scale, k + 1)
+            if k == -1:
+                weight_scale(wa_banks, s_a, wa_grouped)
+                weight_quantize(wa_grouped, wa_codes, wa_scales)
+            stage(h_group, k - 2)
+            stage(square_sums, k)
+            stage(x_transposes, k + 2)
+            if k == 0:
+                wb_banks = weight_transposes(wb_raw, "o", ident)
+                weight_scale(wb_banks, s_b, wb_grouped)
+            if k == 1:
+                weight_quantize(wb_grouped, wb_codes, wb_scales)
+            stage(norm, k - 1)
+            stage(h_transposes, k - 1)
+            stage(finish, k - 3)

@@ -21,6 +21,8 @@ PER = 8
 GROUPS = S // (P * PER)
 PAIRS = S // (2 * P)
 PAIRS_G = PER // 2
+S_CAST_HEAD = 4
+V_OUT_TAIL = 6
 
 
 def tile_deepseekv3attention_pb_t_kernel(
@@ -97,7 +99,7 @@ def tile_deepseekv3attention_pb_t_kernel(
                     n0 = 256 * a + 64 * b
                     part = src[:, :, 128 * a : 128 * a + 128].rearrange("p u (n e) -> p n u e", e=2)
                     dst = grouped[:, n0 : n0 + 64, :].rearrange("p n (u e) -> p n u e", e=2)
-                    if a == 0:
+                    if a == 0 or s_col is s_b:
                         nc.scalar.activation(out=dst, in_=part, func=ACT.Copy, scale=s_col[:, b : b + 1])
                     else:
                         nc.vector.tensor_scalar(out=dst, in0=part, scalar1=s_col[:, b : b + 1], scalar2=None, op0=MULT)
@@ -117,13 +119,13 @@ def tile_deepseekv3attention_pb_t_kernel(
         st = {}
 
         def widen(k):
-            g, j = divmod(k, PAIRS_G)
+            g, i = divmod(k, PAIRS_G)
             xb = ring.tile([P, 2 * HID], BF16, name="xb", bufs=3, align_bytes=64)
-            src = x_bytes[:, g, 2 * j : 2 * j + 2, :].rearrange("p j k -> p (j k)").bitcast(E4M3)
-            if k == 0:
-                nc.vector.tensor_copy(out=xb[:], in_=src)
+            src = x_bytes[:, g, 2 * i : 2 * i + 2, :].rearrange("p j k -> p (j k)").bitcast(E4M3)
+            if k < S_CAST_HEAD or k % 2 == 1:
+                nc.scalar.copy(out=xb[:], in_=src)
             else:
-                nc.gpsimd.tensor_copy(out=xb[:], in_=src)
+                nc.vector.tensor_copy(out=xb[:], in_=src)
             st["xb", k] = xb
 
         def x_transposes(k):
@@ -136,7 +138,7 @@ def tile_deepseekv3attention_pb_t_kernel(
 
         def x_scale(k):
             xt = st.pop(("xt", k))
-            xg = ring.tile([P, 2 * P, 4], BF16, name="xg", bufs=2, align_bytes=64)
+            xg = ring.tile([P, 2 * P, 4], BF16, name="xg", bufs=3, align_bytes=64)
             nc.vector.tensor_tensor(
                 out=xg[:].rearrange("p r (u e) -> p r u e", e=2),
                 in0=xt[:].bitcast(BF16).rearrange("p u (r e) -> p r u e", e=2),
@@ -147,16 +149,21 @@ def tile_deepseekv3attention_pb_t_kernel(
 
         def quantize(k, src, dst):
             grouped = st.pop((src, k))
-            codes = ring.tile([P, 2 * P], U32, name=dst + "c", bufs=2, align_bytes=64)
-            scales = ring.tile([P, 2 * P], U8, name=dst + "s", bufs=2, align_bytes=64)
+            codes = ring.tile([P, 2 * P], U32, name=dst + "c", bufs=3, align_bytes=64)
+            scales = ring.tile([P, 2 * P], U8, name=dst + "s", bufs=3, align_bytes=64)
             nc.vector.quantize_mx(
                 out=codes[:].bitcast(FP8X4), scales=scales[:], in_=grouped[:].rearrange("p r t -> p (r t)")
             )
             st[dst, k] = (codes, scales)
 
+        def x_quantize(k):
+            quantize(k, "xg", "xq")
+
+        def h_quantize(k):
+            quantize(k, "hg", "hq")
+
         def multiply(k, src, w_codes, w_scales, dst, bufs):
             codes, scales = st.pop((src, k))
-            res = []
             for j in range(2):
                 cols = slice(P * j, P * j + P)
                 acc = psum.tile([P, 512], F32, name=dst, bufs=bufs)
@@ -169,30 +176,41 @@ def tile_deepseekv3attention_pb_t_kernel(
                     start=True,
                     stop=True,
                 )
-                res.append(acc)
-            st[dst, k] = res
+                st[dst, k, j] = acc
+
+        def down(k):
+            multiply(k, "xq", wa_codes, wa_scales, "c", 4)
+
+        def up(k):
+            multiply(k, "hq", wb_codes, wb_scales, "o", 2)
 
         def square_sums(k):
-            junk = ring.tile([P, LAT], BF16, name="junk", bufs=2)
-            ssq = ring.tile([P, 2], F32, name="ssq", bufs=3)
-            rstd = ring.tile([P, 2], F32, name="rstd", bufs=3)
+            ssq = ring.tile([P, 2], F32, name="ssq", bufs=4)
             for j in range(2):
+                junk = ring.tile([P, LAT], BF16, name="junk", bufs=2)
                 nc.scalar.activation(
-                    out=junk[:], in_=st["c", k][j][:], func=ACT.Square, accum_out=ssq[:, j : j + 1]
+                    out=junk[:], in_=st["c", k, j][:], func=ACT.Square, accum_out=ssq[:, j : j + 1]
                 )
+            st["ssq", k] = ssq
+
+        def inverse_rms(k):
+            rstd = ring.tile([P, 2], F32, name="rstd", bufs=4)
             nc.scalar.activation(
-                out=rstd[:], in_=ssq[:], func=ACT.Abs_reciprocal_sqrt, scale=1.0 / LAT, bias=eps[:, 0:1]
+                out=rstd[:], in_=st.pop(("ssq", k))[:], func=ACT.Abs_reciprocal_sqrt, scale=1.0 / LAT, bias=eps[:, 0:1]
             )
             st["rstd", k] = rstd
 
-        def norm(k):
-            rstd = st.pop(("rstd", k))
-            h = ring.tile([P, 2, LAT], BF16, name="h", bufs=2, align_bytes=64)
-            for j, acc in enumerate(st.pop(("c", k))):
-                nc.vector.scalar_tensor_tensor(
-                    out=h[:, j, :], in0=acc[:], scalar=rstd[:, j : j + 1], in1=gain[:], op0=MULT, op1=MULT
-                )
-            st["h", k] = h
+        def norm(k, j):
+            if j == 0:
+                st["h", k] = ring.tile([P, 2, LAT], BF16, name="h", bufs=3, align_bytes=64)
+            nc.vector.scalar_tensor_tensor(
+                out=st["h", k][:, j, :],
+                in0=st.pop(("c", k, j))[:],
+                scalar=st["rstd", k][:, j : j + 1],
+                in1=gain[:],
+                op0=MULT,
+                op1=MULT,
+            )
 
         def h_transposes(k):
             words = st.pop(("h", k))[:].bitcast(F32)
@@ -204,42 +222,52 @@ def tile_deepseekv3attention_pb_t_kernel(
 
         def h_group(k):
             ht = st.pop(("ht", k))
-            hg = ring.tile([P, 2 * P, 4], BF16, name="hg", bufs=2, align_bytes=64)
+            hg = ring.tile([P, 2 * P, 4], BF16, name="hg", bufs=3, align_bytes=64)
             nc.scalar.copy(out=hg[:].bitcast(F32), in_=ht[:].rearrange("p u r -> p r u"))
             st["hg", k] = hg
 
-        def finish(k):
+        def finish(k, j):
             g, i = divmod(k, PAIRS_G)
-            res = ring.tile([P, 2, 2, 256], F32, name="res", bufs=3)
-            for j, acc in enumerate(st.pop(("o", k))):
-                nc.scalar.copy(out=res[:, :, j, :], in_=acc[:].rearrange("p (h n) -> p h n", h=2))
-            for half in range(2):
-                nc.sync.dma_start(out=o_hbm[half][g][:, 2 * i : 2 * i + 2, :], in_=res[:, half, :, :])
+            if j == 0:
+                st["res", k] = ring.tile([P, 2, 2, 256], F32, name="res", bufs=4)
+            res = st["res", k]
+            src = st.pop(("o", k, j))[:].rearrange("p (h n) -> p h n", h=2)
+            if j == 1 and k >= PAIRS - V_OUT_TAIL:
+                nc.vector.tensor_copy(out=res[:, :, j, :], in_=src)
+            else:
+                nc.scalar.copy(out=res[:, :, j, :], in_=src)
+            if j == 1:
+                for half in range(2):
+                    nc.sync.dma_start(out=o_hbm[half][g][:, 2 * i : 2 * i + 2, :], in_=res[:, half, :, :])
 
-        def stage(fn, k, *args):
-            if 0 <= k < PAIRS:
-                fn(k, *args)
-
-        for k in range(-3, PAIRS + 3):
-            stage(widen, k + 3)
+        PERIOD = [
+            (h_quantize, -3, ()),
+            (finish, -4, (1,)),
+            (x_scale, 1, ()),
+            (norm, -1, (0,)),
+            (h_transposes, -2, ()),
+            (down, 0, ()),
+            (h_group, -2, ()),
+            (up, -3, ()),
+            (square_sums, 0, ()),
+            (finish, -3, (0,)),
+            (norm, -1, (1,)),
+            (x_quantize, 1, ()),
+            (widen, 3, ()),
+            (inverse_rms, 0, ()),
+            (x_transposes, 2, ()),
+        ]
+        for k in range(-3, PAIRS + 4):
             if k == -1:
                 wa_banks = weight_transposes(wa_raw, "c", ident_a)
-            stage(quantize, k, "xg", "xq")
-            stage(quantize, k - 3, "hg", "hq")
-            stage(multiply, k, "xq", wa_codes, wa_scales, "c", 4)
-            stage(multiply, k - 3, "hq", wb_codes, wb_scales, "o", 2)
-            stage(x_scale, k + 1)
-            if k == -1:
-                weight_scale(wa_banks, s_a, wa_grouped)
-                weight_quantize(wa_grouped, wa_codes, wa_scales)
-            stage(h_group, k - 2)
-            stage(square_sums, k)
-            stage(x_transposes, k + 2)
+            for fn, ahead, args in PERIOD:
+                if 0 <= k + ahead < PAIRS:
+                    fn(k + ahead, *args)
+                if k == -1 and fn is x_scale:
+                    weight_scale(wa_banks, s_a, wa_grouped)
+                    weight_quantize(wa_grouped, wa_codes, wa_scales)
             if k == 0:
                 wb_banks = weight_transposes(wb_raw, "o", ident)
                 weight_scale(wb_banks, s_b, wb_grouped)
             if k == 1:
                 weight_quantize(wb_grouped, wb_codes, wb_scales)
-            stage(norm, k - 1)
-            stage(h_transposes, k - 1)
-            stage(finish, k - 3)

from contextlib import ExitStack

import concourse.mybir as mybir
from concourse.masks import make_identity

S, HID, LAT, OUT = 8192, 512, 512, 512
EPS = 1e-6
FLOPS = 2 * S * HID * LAT + 2 * S * LAT * OUT

F32 = mybir.dt.float32
BF16 = mybir.dt.bfloat16
U32 = mybir.dt.uint32
U8 = mybir.dt.uint8
E4M3 = mybir.dt.float8_e4m3fn
FP8X4 = mybir.dt.float8_e4m3fn_x4
ACT = mybir.ActivationFunctionType
MULT = mybir.AluOpType.mult

P = 128
PER = 8
GROUPS = S // (P * PER)
PAIRS = S // (2 * P)
PAIRS_G = PER // 2
S_CAST_HEAD = 4
V_OUT_TAIL = 6


def tile_deepseekv3attention_pb_t_kernel(
    tc, hidden_states_bytes, hidden_states_scale, wkv_a_lat, skv_a_lat, wkv_b, skv_b, kv_ln_w, out_0, out_1
):
    nc = tc.nc
    x_hbm = hidden_states_bytes.rearrange("(g p j) k -> g p j k", p=P, j=PER)
    o_hbm = [
        o.rearrange("(g p j) h d -> g p j (h d)", p=P, j=PER) for o in (out_0, out_1)
    ]

    with ExitStack() as ctx:
        keep = ctx.enter_context(tc.tile_pool(name="keep", bufs=1))
        ring = ctx.enter_context(tc.tile_pool(name="ring", bufs=3))
        psum = ctx.enter_context(tc.psum_pool(name="psum", bufs=1))
        ctx.enter_context(tc.manual_schedule())

        x_bytes = keep.tile([P, GROUPS, PER, HID], U8, align_bytes=64)
        nc.sync.dma_start(out=x_bytes[:, 0, 0:2, :], in_=x_hbm[0][:, 0:2, :])
        wa_raw = keep.tile([P, 4, HID], BF16, align_bytes=64)
        nc.sync.dma_start(out=wa_raw[:], in_=wkv_a_lat.rearrange("(b q) k -> q b k", q=P))
        k_scale = keep.tile([P, 4], F32)
        nc.scalar.dma_start(out=k_scale[:], in_=hidden_states_scale.rearrange("o (p t) -> p (o t)", t=4))
        skv_a_row = keep.tile([P, 16], BF16)
        nc.scalar.dma_start(out=skv_a_row[:], in_=skv_a_lat.rearrange("b g -> (b g)").partition_broadcast(P))
        nc.sync.dma_start(out=x_bytes[:, 0, 2:PER, :], in_=x_hbm[0][:, 2:PER, :])
        wb_raw = keep.tile([P, 4, LAT], BF16, align_bytes=64)
        nc.sync.dma_start(out=wb_raw[:], in_=wkv_b.rearrange("(b q) k -> q b k", q=P))
        skv_b_row = keep.tile([P, 16], BF16)
        nc.scalar.dma_start(out=skv_b_row[:], in_=skv_b.rearrange("b g -> (b g)").partition_broadcast(P))
        gain_row = keep.tile([P, LAT], BF16)
        nc.scalar.dma_start(out=gain_row[:], in_=kv_ln_w.partition_broadcast(P))
        for g in range(1, GROUPS):
            nc.sync.dma_start(out=x_bytes[:, g, :, :], in_=x_hbm[g])

        ident = keep.tile([P, P], F32)
        make_identity(nc, ident[:])
        eps = keep.tile([P, 1], F32)
        nc.vector.memset(eps[:], EPS)
        warm = keep.tile([P, 1], F32)
        nc.scalar.activation(out=warm[:], in_=eps[:], func=ACT.Abs_reciprocal_sqrt, bias=eps[:, 0:1])
        ident_a = keep.tile([P, P], F32)
        nc.gpsimd.tensor_copy(
            out=ident_a[:].rearrange("p (al m ep) -> p al m ep", al=2, ep=2),
            in_=ident[:].rearrange("p (m al ep) -> p al m ep", al=2, ep=2),
        )
        s_a = keep.tile([P, 4], F32)
        s_b = keep.tile([P, 4], F32)
        for s_col, row in ((s_a, skv_a_row), (s_b, skv_b_row)):
            for q in range(4):
                rows = slice(32 * q, 32 * q + 32)
                nc.gpsimd.tensor_copy(out=s_col[rows, :], in_=row[rows, q::4])
        gain = keep.tile([P, LAT], F32)
        nc.gpsimd.tensor_copy(
            out=gain[:].rearrange("p (al m ep) -> p al m ep", al=2, ep=2),
            in_=gain_row[:].rearrange("p (m al ep) -> p al m ep", al=2, ep=2),
        )

        def weight_transposes(raw, tag, identity):
            words = raw[:].bitcast(F32)
            banks = []
            for half in range(2):
                bank = psum.tile([P, 2, 2, P], F32, name=tag, tag=tag, bufs=4 if tag == "c" else 2)
                for h in range(2):
                    for u in range(2):
                        nc.tensor.transpose(bank[:, h, u, :], words[:, 2 * half + h, u::2], identity[:])
                banks.append(bank)
            return banks

        def weight_scale(banks, s_col, grouped):
            for b in range(4):
                src = banks[b // 2][:, b % 2, :, :].bitcast(BF16)
                for a in range(2):
                    n0 = 256 * a + 64 * b
                    part = src[:, :, 128 * a : 128 * a + 128].rearrange("p u (n e) -> p n u e", e=2)
                    dst = grouped[:, n0 : n0 + 64, :].rearrange("p n (u e) -> p n u e", e=2)
                    if a == 0 or s_col is s_b:
                        nc.scalar.activation(out=dst, in_=part, func=ACT.Copy, scale=s_col[:, b : b + 1])
                    else:
                        nc.vector.tensor_scalar(out=dst, in0=part, scalar1=s_col[:, b : b + 1], scalar2=None, op0=MULT)

        def weight_quantize(grouped, codes, scales):
            nc.vector.quantize_mx(
                out=codes[:].bitcast(FP8X4), scales=scales[:], in_=grouped[:].rearrange("p n t -> p (n t)")
            )

        wa_grouped = keep.tile([P, LAT, 4], BF16, align_bytes=64)
        wa_codes = keep.tile([P, LAT], U32, align_bytes=64)
        wa_scales = keep.tile([P, LAT], U8, align_bytes=64)
        wb_grouped = keep.tile([P, OUT, 4], BF16, align_bytes=64)
        wb_codes = keep.tile([P, OUT], U32, align_bytes=64)
        wb_scales = keep.tile([P, OUT], U8, align_bytes=64)

        st = {}

        def widen(k):
            g, i = divmod(k, PAIRS_G)
            xb = ring.tile([P, 2 * HID], BF16, name="xb", bufs=3, align_bytes=64)
            src = x_bytes[:, g, 2 * i : 2 * i + 2, :].rearrange("p j k -> p (j k)").bitcast(E4M3)
            if k < S_CAST_HEAD or k % 2 == 1:
                nc.scalar.copy(out=xb[:], in_=src)
            else:
                nc.vector.tensor_copy(out=xb[:], in_=src)
            st["xb", k] = xb

        def x_transposes(k):
            words = st.pop(("xb", k))[:].bitcast(F32).rearrange("p (j w) -> p j w", j=2)
            xt = psum.tile([P, 2, 2 * P], F32, name="xt", bufs=1)
            for j in range(2):
                for u in range(2):
                    nc.tensor.transpose(xt[:, u, P * j : P * j + P], words[:, j, u::2], ident[:])
            st["xt", k] = xt

        def x_scale(k):
            xt = st.pop(("xt", k))
            xg = ring.tile([P, 2 * P, 4], BF16, name="xg", bufs=3, align_bytes=64)
            nc.vector.tensor_tensor(
                out=xg[:].rearrange("p r (u e) -> p r u e", e=2),
                in0=xt[:].bitcast(BF16).rearrange("p u (r e) -> p r u e", e=2),
                in1=k_scale[:].rearrange("p (u e) -> p u e", e=2).unsqueeze(1).to_broadcast([P, 2 * P, 2, 2]),
                op=MULT,
            )
            st["xg", k] = xg

        def quantize(k, src, dst):
            grouped = st.pop((src, k))
            codes = ring.tile([P, 2 * P], U32, name=dst + "c", bufs=3, align_bytes=64)
            scales = ring.tile([P, 2 * P], U8, name=dst + "s", bufs=3, align_bytes=64)
            nc.vector.quantize_mx(
                out=codes[:].bitcast(FP8X4), scales=scales[:], in_=grouped[:].rearrange("p r t -> p (r t)")
            )
            st[dst, k] = (codes, scales)

        def x_quantize(k):
            quantize(k, "xg", "xq")

        def h_quantize(k):
            quantize(k, "hg", "hq")

        def multiply(k, src, w_codes, w_scales, dst, bufs):
            codes, scales = st.pop((src, k))
            for j in range(2):
                cols = slice(P * j, P * j + P)
                acc = psum.tile([P, 512], F32, name=dst, bufs=bufs)
                nc.tensor.matmul_mx(
                    out=acc[:],
                    lhsT=codes[:, cols].bitcast(FP8X4),
                    lhsT_scale=scales[:, cols],
                    rhs=w_codes[:].bitcast(FP8X4),
                    rhs_scale=w_scales[:],
                    start=True,
                    stop=True,
                )
                st[dst, k, j] = acc

        def down(k):
            multiply(k, "xq", wa_codes, wa_scales, "c", 4)

        def up(k):
            multiply(k, "hq", wb_codes, wb_scales, "o", 2)

        def square_sums(k):
            ssq = ring.tile([P, 2], F32, name="ssq", bufs=4)
            for j in range(2):
                junk = ring.tile([P, LAT], BF16, name="junk", bufs=2)
                nc.scalar.activation(
                    out=junk[:], in_=st["c", k, j][:], func=ACT.Square, accum_out=ssq[:, j : j + 1]
                )
            st["ssq", k] = ssq

        def inverse_rms(k):
            rstd = ring.tile([P, 2], F32, name="rstd", bufs=4)
            nc.scalar.activation(
                out=rstd[:], in_=st.pop(("ssq", k))[:], func=ACT.Abs_reciprocal_sqrt, scale=1.0 / LAT, bias=eps[:, 0:1]
            )
            st["rstd", k] = rstd

        def norm(k, j):
            if j == 0:
                st["h", k] = ring.tile([P, 2, LAT], BF16, name="h", bufs=3, align_bytes=64)
            nc.vector.scalar_tensor_tensor(
                out=st["h", k][:, j, :],
                in0=st.pop(("c", k, j))[:],
                scalar=st["rstd", k][:, j : j + 1],
                in1=gain[:],
                op0=MULT,
                op1=MULT,
            )

        def h_transposes(k):
            words = st.pop(("h", k))[:].bitcast(F32)
            ht = psum.tile([P, 2, 2 * P], F32, name="ht", bufs=1)
            for j in range(2):
                for u in range(2):
                    nc.tensor.transpose(ht[:, u, P * j : P * j + P], words[:, j, P * u : P * u + P], ident[:])
            st["ht", k] = ht

        def h_group(k):
            ht = st.pop(("ht", k))
            hg = ring.tile([P, 2 * P, 4], BF16, name="hg", bufs=3, align_bytes=64)
            nc.scalar.copy(out=hg[:].bitcast(F32), in_=ht[:].rearrange("p u r -> p r u"))
            st["hg", k] = hg

        def finish(k, j):
            g, i = divmod(k, PAIRS_G)
            if j == 0:
                st["res", k] = ring.tile([P, 2, 2, 256], F32, name="res", bufs=4)
            res = st["res", k]
            src = st.pop(("o", k, j))[:].rearrange("p (h n) -> p h n", h=2)
            if j == 1 and k >= PAIRS - V_OUT_TAIL:
                nc.vector.tensor_copy(out=res[:, :, j, :], in_=src)
            else:
                nc.scalar.copy(out=res[:, :, j, :], in_=src)
            if j == 1:
                for half in range(2):
                    nc.sync.dma_start(out=o_hbm[half][g][:, 2 * i : 2 * i + 2, :], in_=res[:, half, :, :])

        PERIOD = [
            (h_quantize, -3, ()),
            (finish, -4, (1,)),
            (x_scale, 1, ()),
            (norm, -1, (0,)),
            (h_transposes, -2, ()),
            (down, 0, ()),
            (h_group, -2, ()),
            (up, -3, ()),
            (square_sums, 0, ()),
            (finish, -3, (0,)),
            (norm, -1, (1,)),
            (x_quantize, 1, ()),
            (widen, 3, ()),
            (inverse_rms, 0, ()),
            (x_transposes, 2, ()),
        ]
        for k in range(-3, PAIRS + 4):
            if k == -1:
                wa_banks = weight_transposes(wa_raw, "c", ident_a)
            for fn, ahead, args in PERIOD:
                if 0 <= k + ahead < PAIRS:
                    fn(k + ahead, *args)
                if k == -1 and fn is x_scale:
                    weight_scale(wa_banks, s_a, wa_grouped)
                    weight_quantize(wa_grouped, wa_codes, wa_scales)
            if k == 0:
                wb_banks = weight_transposes(wb_raw, "o", ident)
                weight_scale(wb_banks, s_b, wb_grouped)
            if k == 1:
                weight_quantize(wb_grouped, wb_codes, wb_scales)
